import numpy as np
import ml_dtypes


def mxq(x, axis, fmt="e4m3"):
    dtype, down = {"e4m3": (ml_dtypes.float8_e4m3fn, 7), "e5m2": (ml_dtypes.float8_e5m2, 14)}[fmt]
    v = np.moveaxis(np.asarray(x, np.float32).astype(ml_dtypes.bfloat16).astype(np.float64), axis, -1)
    blocks = v.reshape(v.shape[:-1] + (-1, 32))
    amax = np.abs(blocks).max(-1, keepdims=True)
    byte = np.maximum(np.where(amax > 0, np.frexp(amax)[1] - 1 + 127, 0) - down, 1)
    scale = np.exp2(byte - 127.0)
    codes = (blocks / scale).astype(np.float32).astype(dtype).astype(np.float64)
    return np.moveaxis((codes * scale).reshape(v.shape), -1, axis)


WIDE = False


def mx_kscale(k):
    if not WIDE:
        return np.ones(k)
    levels = np.array([10, -10, 5, -5, 0])
    a = np.random.permutation(np.resize(levels, k // 512 * 4)).reshape(k // 512, 4)
    idx = np.arange(k)
    return np.exp2(a[idx // 512, idx % 128 // 32])


BF16 = ml_dtypes.bfloat16


def bf(x):
    return np.asarray(x, np.float32).astype(BF16)


def f64(x):
    return np.asarray(x).astype(np.float64)


T, B, D_IN, D_H, D_K, D_OUT = 2, 4096, 512, 1024, 512, 256


def setup_inputs():
    s, t = mx_kscale(D_H), mx_kscale(D_K)
    return {"h1": bf(np.maximum(np.random.standard_normal((T, B, D_H)), 0.0) * s),
            "W2": bf(np.random.standard_normal((T, D_H, D_K)) * 1.4 / np.sqrt(D_H) / s[:, None] * t),
            "b2": bf(np.random.standard_normal((T, D_K)) * 0.2 * t),
            "W3": bf(np.random.standard_normal((T, D_K, D_OUT)) * 1.4 / np.sqrt(D_K) / t[:, None]),
            "b3": bf(np.random.standard_normal((T, D_OUT)) * 0.2)}


def reference(h1, W2, b2, W3, b3):
    h2 = np.maximum((mxq(f64(h1), 2, "e4m3") @ mxq(f64(W2), 1, "e4m3")) + f64(b2)[:, None, :], 0.0)
    out = (mxq(h2, 2, "e4m3") @ mxq(f64(W3), 1, "e4m3")) + f64(b3)[:, None, :]
    return out.mean(axis=0)

@@ -1,0 +1,289 @@
+from contextlib import ExitStack
+
+import concourse.mybir as mybir
+from concourse.masks import make_identity
+
+F32 = mybir.dt.float32
+BF16 = mybir.dt.bfloat16
+U32 = mybir.dt.uint32
+U8 = mybir.dt.uint8
+FP8X4 = mybir.dt.float8_e4m3fn_x4
+ACT = mybir.ActivationFunctionType
+ALU = mybir.AluOpType
+
+T, B, D_H, D_K, D_OUT = 2, 4096, 1024, 512, 256
+P = 128
+CH = 512
+NCH = B // CH
+R = T * NCH
+FLOPS = 2 * T * B * D_H * D_K + 2 * T * B * D_K * D_OUT
+
+NX = 8
+AHEAD = 6
+V_XT = {}
+
+
+def tile_randomforestmlp_pa_t_kernel(tc, h1, W2, b2, W3, b3, out):
+    nc = tc.nc
+    with ExitStack() as ctx:
+        const = ctx.enter_context(tc.tile_pool(name="const", bufs=1))
+        xin = ctx.enter_context(tc.tile_pool(name="xin", bufs=NX))
+        wst = ctx.enter_context(tc.tile_pool(name="wst", bufs=2))
+        ghp = ctx.enter_context(tc.tile_pool(name="ghp", bufs=4))
+        hcp = ctx.enter_context(tc.tile_pool(name="hcp", bufs=3))
+        h2p = ctx.enter_context(tc.tile_pool(name="h2p", bufs=2))
+        h2cp = ctx.enter_context(tc.tile_pool(name="h2cp", bufs=4))
+        outp = ctx.enter_context(tc.tile_pool(name="outp", bufs=3))
+        ps_tr = ctx.enter_context(tc.psum_pool(name="ps_tr", bufs=4))
+        ps_s1 = ctx.enter_context(tc.psum_pool(name="ps_s1", bufs=3))
+        ps_s2 = ctx.enter_context(tc.psum_pool(name="ps_s2", bufs=1))
+        ctx.enter_context(tc.manual_schedule())
+
+        xs = {}
+
+        def load_x(r):
+            c, t = r // 2, r % 2
+            x = xin.tile([P, 4 * D_H], BF16, name="x", tag="x")
+            nc.sync.dma_start(
+                out=x[:].rearrange("p (j k) -> p j k", j=4),
+                in_=h1[t, c * CH : (c + 1) * CH, :].rearrange("(p j) k -> p j k", j=4),
+            )
+            xs[r] = x
+
+        w2raw = {}
+        w3raw = {}
+
+        def load_w2(t):
+            w = const.tile([P, 8, D_K], BF16, name="w2raw%d" % t)
+            nc.sync.dma_start(
+                out=w[:].rearrange("p (a e) w -> p a e w", e=2),
+                in_=W2[t].rearrange("(a p e) w -> p a e w", a=4, p=P, e=2),
+            )
+            w2raw[t] = w
+
+        def load_w3(t):
+            w = const.tile([P, 4, D_OUT], BF16, name="w3raw%d" % t)
+            nc.sync.dma_start(out=w[:], in_=W3[t].rearrange("(m p) o -> p m o", p=P))
+            w3raw[t] = w
+
+        b2rows = const.tile([P, P], BF16, name="b2rows")
+        nc.vector.memset(b2rows[:], 0.0)
+        nc.scalar.dma_start(out=b2rows[0:8, :], in_=b2.rearrange("t (m i) -> (t m) i", i=P))
+        b3rows = const.tile([P, D_OUT], BF16, name="b3rows")
+        nc.vector.memset(b3rows[:], 0.0)
+        nc.scalar.dma_start(out=b3rows[0:2, :], in_=b3)
+        halves = const.tile([P, P], BF16, name="halves")
+        nc.vector.memset(halves[:], 0.5)
+
+        load_w2(0)
+        load_x(0)
+        load_x(1)
+        load_w2(1)
+        load_w3(0)
+        load_w3(1)
+        for r in range(2, AHEAD):
+            load_x(r)
+
+        ident = const.tile([P, P], F32, name="ident")
+        make_identity(nc, ident[:])
+        ident_bf = const.tile([P, P], BF16, name="ident_bf")
+        nc.vector.tensor_copy(out=ident_bf[:], in_=ident[:])
+
+        pb2 = ps_tr.tile([P, P], BF16, name="pb2", tag="tr")
+        nc.tensor.transpose(out=pb2[:], in_=b2rows[:], identity=ident_bf[:])
+        bias2 = const.tile([P, 8], F32, name="bias2")
+        nc.vector.tensor_copy(out=bias2[:], in_=pb2[:, 0:8])
+        pb3 = ps_tr.tile([P, D_OUT], F32, name="pb3", tag="tr")
+        nc.tensor.matmul(out=pb3[:], lhsT=halves[:], rhs=b3rows[:], start=True, stop=True)
+        b3bc = const.tile([P, 2, D_OUT], F32, name="b3bc")
+        nc.vector.tensor_copy(out=b3bc[:, 0, :], in_=pb3[:])
+        nc.vector.tensor_copy(out=b3bc[:, 1, :], in_=pb3[:])
+
+        w2c = {}
+        w2s = {}
+        w3c = {}
+        w3s = {}
+        for t in range(T):
+            w2c[t] = const.tile([P, 2, D_K], U32, name="w2c%d" % t, align_bytes=64)
+            w2s[t] = const.tile([P, 2, D_K], U8, name="w2s%d" % t, align_bytes=64)
+            w3c[t] = const.tile([P, D_OUT], U32, name="w3c%d" % t, align_bytes=64)
+            w3s[t] = const.tile([P, D_OUT], U8, name="w3s%d" % t, align_bytes=64)
+
+        def prep_w2(t):
+            grp = {}
+            for g in range(2):
+                wg = wst.tile([P, 4 * D_K], BF16, name="wg", tag="wg", align_bytes=64)
+                nc.vector.tensor_copy(
+                    out=wg[:].rearrange("p (c i t) -> p c t i", i=4, t=4),
+                    in_=w2raw[t][:, 4 * g : 4 * g + 4, :].rearrange("p t (c i) -> p c t i", i=4),
+                )
+                grp[g] = wg
+            for g in range(2):
+                nc.vector.quantize_mx(
+                    out=w2c[t][:, g, :].bitcast(FP8X4), scales=w2s[t][:, g, :], in_=grp[g][:]
+                )
+
+        def prep_w3():
+            grp = {}
+            for t in range(T):
+                wg = wst.tile([P, 4 * D_OUT], BF16, name="wg3", tag="wg", align_bytes=64)
+                nc.vector.tensor_copy(
+                    out=wg[:].rearrange("p (c i t) -> p c t i", i=4, t=4),
+                    in_=w3raw[t][:].rearrange("p t (c i) -> p c t i", i=4),
+                )
+                grp[t] = wg
+            for t in range(T):
+                nc.vector.quantize_mx(out=w3c[t][:].bitcast(FP8X4), scales=w3s[t][:], in_=grp[t][:])
+
+        trb = {}
+        ghs = {}
+        hcs = {}
+        h2ts = {}
+        g2s = {}
+        h2cs = {}
+        pos = {}
+        osb = {}
+
+        def transposes(r):
+            xw = xs[r][:].bitcast(F32)
+            for g in range(2):
+                for h in range(2):
+                    bank = ps_tr.tile([P, 2, 256], F32, name="trb", tag="tr")
+                    for u in range(2):
+                        for jj in range(2):
+                            col = (2 * h + jj) * 512 + g * 256 + u * 128
+                            nc.tensor.transpose(
+                                out=bank[:, u, jj * P : (jj + 1) * P],
+                                in_=xw[:, col : col + P],
+                                identity=ident[:],
+                            )
+                    trb[(r, g, h)] = bank
+
+        def exit_t(r, i):
+            g, h = i // 2, i % 2
+            if h == 0:
+                gh = ghp.tile([P, 4 * CH], BF16, name="gh", tag="gh", align_bytes=64)
+                ghs[(r, g)] = gh
+            dst = ghs[(r, g)][:].bitcast(F32).rearrange("p (n u) -> p n u", u=2)
+            dst = dst[:, 256 * h : 256 * h + 256, :]
+            src = trb[(r, g, h)][:].rearrange("p u n -> p n u")
+            if i in V_XT.get(r % 2, ()):
+                nc.vector.tensor_copy(out=dst, in_=src)
+            else:
+                nc.scalar.copy(out=dst, in_=src)
+
+        def quant_h1(r, g):
+            if g == 0:
+                hc = hcp.tile([P, 2, CH], U32, name="hc", tag="hc", align_bytes=64)
+                hs = hcp.tile([P, 2, CH], U8, name="hs", tag="hs", align_bytes=64)
+                hcs[r] = (hc, hs)
+            hc, hs = hcs[r]
+            nc.vector.quantize_mx(
+                out=hc[:, g, :].bitcast(FP8X4), scales=hs[:, g, :], in_=ghs[(r, g)][:]
+            )
+
+        def stage1(r, m):
+            t = r % 2
+            hc, hs = hcs[r]
+            if m == 0:
+                h2t = h2p.tile([P, 4, CH], BF16, name="h2t", tag="h2t")
+                h2ts[r] = h2t
+            ps = ps_s1.tile([P, CH], F32, name="ps1", tag="s1")
+            for g in range(2):
+                nc.tensor.matmul_mx(
+                    out=ps[:],
+                    lhsT=w2c[t][:, g, m * P : (m + 1) * P].bitcast(FP8X4),
+                    lhsT_scale=w2s[t][:, g, m * P : (m + 1) * P],
+                    rhs=hc[:, g, :].bitcast(FP8X4),
+                    rhs_scale=hs[:, g, :],
+                    start=(g == 0),
+                    stop=(g == 1),
+                )
+            nc.scalar.activation(
+                out=h2ts[r][:, m, :],
+                in_=ps[:],
+                func=ACT.Relu,
+                bias=bias2[:, 4 * t + m : 4 * t + m + 1],
+                scale=1.0,
+            )
+
+        def regroup(r):
+            g2 = h2p.tile([P, 4 * CH], BF16, name="g2", tag="g2", align_bytes=64)
+            nc.vector.tensor_copy(
+                out=g2[:].rearrange("p (c i t) -> p c t i", i=4, t=4),
+                in_=h2ts[r][:].rearrange("p t (c i) -> p c t i", i=4),
+            )
+            g2s[r] = g2
+
+        def quant_h2(r):
+            h2c = h2cp.tile([P, CH], U32, name="h2c", tag="h2c", align_bytes=64)
+            h2s = h2cp.tile([P, CH], U8, name="h2s", tag="h2s", align_bytes=64)
+            nc.vector.quantize_mx(out=h2c[:].bitcast(FP8X4), scales=h2s[:], in_=g2s[r][:])
+            h2cs[r] = (h2c, h2s)
+
+        def stage2(c, hf):
+            po = ps_s2.tile([P, 2, D_OUT], F32, name="po", tag="s2")
+            for jj in range(2):
+                j = 2 * hf + jj
+                for t in range(T):
+                    h2c, h2s = h2cs[2 * c + t]
+                    nc.tensor.matmul_mx(
+                        out=po[:, jj, :],
+                        lhsT=h2c[:, j * P : (j + 1) * P].bitcast(FP8X4),
+                        lhsT_scale=h2s[:, j * P : (j + 1) * P],
+                        rhs=w3c[t][:].bitcast(FP8X4),
+                        rhs_scale=w3s[t][:],
+                        start=(t == 0),
+                        stop=(t == T - 1),
+                    )
+            pos[(c, hf)] = po
+
+        def exit_o(c, hf):
+            if hf == 0:
+                o = outp.tile([P, 4, D_OUT], F32, name="o", tag="o")
+                osb[c] = o
+            nc.vector.scalar_tensor_tensor(
+                out=osb[c][:, 2 * hf : 2 * hf + 2, :],
+                in0=pos[(c, hf)][:],
+                scalar=0.5,
+                in1=b3bc[:],
+                op0=ALU.mult,
+                op1=ALU.add,
+            )
+            if hf == 1:
+                nc.sync.dma_start(
+                    out=out[c * CH : (c + 1) * CH, :].rearrange("(p j) o -> p j o", j=4),
+                    in_=osb[c][:],
+                )
+
+        prep_w2(0)
+        pending = None
+        for s in range(R + 5):
+            if s + AHEAD < R:
+                load_x(s + AHEAD)
+            r1, r2, a = s - 1, s - 2, s - 3
+            if s < R:
+                transposes(s)
+            if 0 <= r2 < R:
+                regroup(r2)
+            if pending is not None:
+                exit_o(pending[0], pending[1])
+                pending = None
+            if 0 <= r2 < R:
+                quant_h2(r2)
+            if s < R:
+                for i in range(4):
+                    exit_t(s, i)
+            if 0 <= r1 < R:
+                for m in range(4):
+                    stage1(r1, m)
+            if s < R:
+                quant_h1(s, 0)
+                quant_h1(s, 1)
+            if s == 0:
+                prep_w2(1)
+            if s == 1:
+                prep_w3()
+            if 0 <= a < R:
+                stage2(a // 2, a % 2)
+                pending = (a // 2, a % 2)

@@ -14,17 +14,27 @@ ALU = mybir.AluOpType
 T, B, D_H, D_K, D_OUT = 2, 4096, 1024, 512, 256
 P = 128
 CH = 512
+HALF = 256
 NCH = B // CH
-R = T * NCH
 FLOPS = 2 * T * B * D_H * D_K + 2 * T * B * D_K * D_OUT
 
 NX = 8
 AHEAD = 6
-V_XT = {}
+V_FROM = 5
 
 
 def tile_randomforestmlp_pa_t_kernel(tc, h1, W2, b2, W3, b3, out):
     nc = tc.nc
+    rounds = [(2 * q + i, t) for q in range(NCH // 2) for t in range(T) for i in range(2)]
+    units = []
+    for r, (c, t) in enumerate(rounds):
+        if r == 0 or r == len(rounds) - 1:
+            units.append((c, t, 0, 1))
+            units.append((c, t, 1, 1))
+        else:
+            units.append((c, t, 0, 2))
+    n_units = len(units)
+
     with ExitStack() as ctx:
         const = ctx.enter_context(tc.tile_pool(name="const", bufs=1))
         xin = ctx.enter_context(tc.tile_pool(name="xin", bufs=NX))
@@ -32,7 +42,7 @@ def tile_randomforestmlp_pa_t_kernel(tc, h1, W2, b2, W3, b3, out):
         ghp = ctx.enter_context(tc.tile_pool(name="ghp", bufs=4))
         hcp = ctx.enter_context(tc.tile_pool(name="hcp", bufs=3))
         h2p = ctx.enter_context(tc.tile_pool(name="h2p", bufs=2))
-        h2cp = ctx.enter_context(tc.tile_pool(name="h2cp", bufs=4))
+        h2cp = ctx.enter_context(tc.tile_pool(name="h2cp", bufs=6))
         outp = ctx.enter_context(tc.tile_pool(name="outp", bufs=3))
         ps_tr = ctx.enter_context(tc.psum_pool(name="ps_tr", bufs=4))
         ps_s1 = ctx.enter_context(tc.psum_pool(name="ps_s1", bufs=3))
@@ -41,24 +51,32 @@ def tile_randomforestmlp_pa_t_kernel(tc, h1, W2, b2, W3, b3, out):
 
         xs = {}
 
-        def load_x(r):
-            c, t = r // 2, r % 2
+        def load_x(r, pieces):
+            c, t = rounds[r]
             x = xin.tile([P, 4 * D_H], BF16, name="x", tag="x")
-            nc.sync.dma_start(
-                out=x[:].rearrange("p (j k) -> p j k", j=4),
-                in_=h1[t, c * CH : (c + 1) * CH, :].rearrange("(p j) k -> p j k", j=4),
-            )
-            xs[r] = x
+            rows = h1[t, c * CH : (c + 1) * CH, :].rearrange("(p j) k -> p j k", j=4)
+            step = 4 // pieces
+            for i in range(pieces):
+                nc.sync.dma_start(
+                    out=x[:, i * step * D_H : (i + 1) * step * D_H].rearrange(
+                        "p (j k) -> p j k", j=step
+                    ),
+                    in_=rows[:, i * step : (i + 1) * step, :],
+                )
+            xs[(c, t)] = x
 
         w2raw = {}
         w3raw = {}
 
         def load_w2(t):
             w = const.tile([P, 8, D_K], BF16, name="w2raw%d" % t)
-            nc.sync.dma_start(
-                out=w[:].rearrange("p (a e) w -> p a e w", e=2),
-                in_=W2[t].rearrange("(a p e) w -> p a e w", a=4, p=P, e=2),
-            )
+            for g in range(2):
+                nc.sync.dma_start(
+                    out=w[:, 4 * g : 4 * g + 4, :].rearrange("p (u e) w -> p u e w", e=2),
+                    in_=W2[t, g * 512 : (g + 1) * 512, :].rearrange(
+                        "(u p e) w -> p u e w", u=2, p=P, e=2
+                    ),
+                )
             w2raw[t] = w
 
         def load_w3(t):
@@ -68,36 +86,48 @@ def tile_randomforestmlp_pa_t_kernel(tc, h1, W2, b2, W3, b3, out):
 
         b2rows = const.tile([P, P], BF16, name="b2rows")
         nc.vector.memset(b2rows[:], 0.0)
-        nc.scalar.dma_start(out=b2rows[0:8, :], in_=b2.rearrange("t (m i) -> (t m) i", i=P))
         b3rows = const.tile([P, D_OUT], BF16, name="b3rows")
         nc.vector.memset(b3rows[:], 0.0)
-        nc.scalar.dma_start(out=b3rows[0:2, :], in_=b3)
         halves = const.tile([P, P], BF16, name="halves")
         nc.vector.memset(halves[:], 0.5)
+        nc.sync.dma_start(out=b2rows[0:8, :], in_=b2.rearrange("t (m i) -> (t m) i", i=P))
+        nc.sync.dma_start(out=b3rows[0:2, :], in_=b3)
 
         load_w2(0)
-        load_x(0)
-        load_x(1)
+        load_x(0, 2)
+        load_x(1, 1)
+        load_x(2, 1)
         load_w2(1)
+        load_x(3, 1)
         load_w3(0)
         load_w3(1)
-        for r in range(2, AHEAD):
-            load_x(r)
+        for r in range(4, AHEAD):
+            load_x(r, 1)
 
         ident = const.tile([P, P], F32, name="ident")
         make_identity(nc, ident[:])
-        ident_bf = const.tile([P, P], BF16, name="ident_bf")
-        nc.vector.tensor_copy(out=ident_bf[:], in_=ident[:])
+        ident_bf = const.tile([P, 32], BF16, name="ident_bf")
+        nc.vector.tensor_copy(out=ident_bf[:], in_=ident[:, 0:32])
 
-        pb2 = ps_tr.tile([P, P], BF16, name="pb2", tag="tr")
-        nc.tensor.transpose(out=pb2[:], in_=b2rows[:], identity=ident_bf[:])
         bias2 = const.tile([P, 8], F32, name="bias2")
-        nc.vector.tensor_copy(out=bias2[:], in_=pb2[:, 0:8])
-        pb3 = ps_tr.tile([P, D_OUT], F32, name="pb3", tag="tr")
-        nc.tensor.matmul(out=pb3[:], lhsT=halves[:], rhs=b3rows[:], start=True, stop=True)
         b3bc = const.tile([P, 2, D_OUT], F32, name="b3bc")
-        nc.vector.tensor_copy(out=b3bc[:, 0, :], in_=pb3[:])
-        nc.vector.tensor_copy(out=b3bc[:, 1, :], in_=pb3[:])
+        pbias = {}
+
+        def bias_matmuls():
+            pb = ps_s2.tile([P, 512], F32, name="pb", tag="s2")
+            nc.tensor.matmul(
+                out=pb[:, 0:D_OUT], lhsT=halves[:], rhs=b3rows[:], start=True, stop=True
+            )
+            nc.tensor.matmul(
+                out=pb[:, D_OUT : D_OUT + 32], lhsT=b2rows[:], rhs=ident_bf[:], start=True, stop=True
+            )
+            pbias[0] = pb
+
+        def bias_copies():
+            pb = pbias[0]
+            nc.vector.tensor_copy(out=bias2[:], in_=pb[:, D_OUT : D_OUT + 8])
+            nc.vector.tensor_copy(out=b3bc[:, 0, :], in_=pb[:, 0:D_OUT])
+            nc.vector.tensor_copy(out=b3bc[:, 1, :], in_=pb[:, 0:D_OUT])
 
         w2c = {}
         w2s = {}
@@ -144,11 +174,12 @@ def tile_randomforestmlp_pa_t_kernel(tc, h1, W2, b2, W3, b3, out):
         pos = {}
         osb = {}
 
-        def transposes(r):
-            xw = xs[r][:].bitcast(F32)
+        def transposes(s):
+            c, t, h0, nh = units[s]
+            xw = xs[(c, t)][:].bitcast(F32)
             for g in range(2):
-                for h in range(2):
-                    bank = ps_tr.tile([P, 2, 256], F32, name="trb", tag="tr")
+                for h in range(h0, h0 + nh):
+                    bank = ps_tr.tile([P, 2, HALF], F32, name="trb", tag="tr")
                     for u in range(2):
                         for jj in range(2):
                             col = (2 * h + jj) * 512 + g * 256 + u * 128
@@ -157,76 +188,90 @@ def tile_randomforestmlp_pa_t_kernel(tc, h1, W2, b2, W3, b3, out):
                                 in_=xw[:, col : col + P],
                                 identity=ident[:],
                             )
-                    trb[(r, g, h)] = bank
+                    trb[(s, g, h)] = bank
 
-        def exit_t(r, i):
-            g, h = i // 2, i % 2
-            if h == 0:
-                gh = ghp.tile([P, 4 * CH], BF16, name="gh", tag="gh", align_bytes=64)
-                ghs[(r, g)] = gh
-            dst = ghs[(r, g)][:].bitcast(F32).rearrange("p (n u) -> p n u", u=2)
-            dst = dst[:, 256 * h : 256 * h + 256, :]
-            src = trb[(r, g, h)][:].rearrange("p u n -> p n u")
-            if i in V_XT.get(r % 2, ()):
-                nc.vector.tensor_copy(out=dst, in_=src)
-            else:
-                nc.scalar.copy(out=dst, in_=src)
-
-        def quant_h1(r, g):
-            if g == 0:
-                hc = hcp.tile([P, 2, CH], U32, name="hc", tag="hc", align_bytes=64)
-                hs = hcp.tile([P, 2, CH], U8, name="hs", tag="hs", align_bytes=64)
-                hcs[r] = (hc, hs)
-            hc, hs = hcs[r]
-            nc.vector.quantize_mx(
-                out=hc[:, g, :].bitcast(FP8X4), scales=hs[:, g, :], in_=ghs[(r, g)][:]
-            )
-
-        def stage1(r, m):
-            t = r % 2
-            hc, hs = hcs[r]
-            if m == 0:
-                h2t = h2p.tile([P, 4, CH], BF16, name="h2t", tag="h2t")
-                h2ts[r] = h2t
-            ps = ps_s1.tile([P, CH], F32, name="ps1", tag="s1")
+        def exits_t(s):
+            c, t, h0, nh = units[s]
             for g in range(2):
-                nc.tensor.matmul_mx(
-                    out=ps[:],
-                    lhsT=w2c[t][:, g, m * P : (m + 1) * P].bitcast(FP8X4),
-                    lhsT_scale=w2s[t][:, g, m * P : (m + 1) * P],
-                    rhs=hc[:, g, :].bitcast(FP8X4),
-                    rhs_scale=hs[:, g, :],
-                    start=(g == 0),
-                    stop=(g == 1),
-                )
-            nc.scalar.activation(
-                out=h2ts[r][:, m, :],
-                in_=ps[:],
-                func=ACT.Relu,
-                bias=bias2[:, 4 * t + m : 4 * t + m + 1],
-                scale=1.0,
-            )
+                gh = ghp.tile([P, 4 * CH], BF16, name="gh", tag="gh", align_bytes=64)
+                ghs[(s, g)] = gh
+                words = gh[:].bitcast(F32).rearrange("p (n u) -> p n u", u=2)
+                for i in range(nh):
+                    dst = words[:, HALF * i : HALF * (i + 1), :]
+                    src = trb[(s, g, h0 + i)][:].rearrange("p u n -> p n u")
+                    if nh == 2 and s >= V_FROM and g == 1 and i == 1:
+                        nc.vector.tensor_copy(out=dst, in_=src)
+                    else:
+                        nc.scalar.copy(out=dst, in_=src)
 
-        def regroup(r):
+        def quant_h1(s):
+            n = HALF * units[s][3]
+            hc = hcp.tile([P, 2, CH], U32, name="hc", tag="hc", align_bytes=64)
+            hs = hcp.tile([P, 2, CH], U8, name="hs", tag="hs", align_bytes=64)
+            hcs[s] = (hc, hs)
+            for g in range(2):
+                nc.vector.quantize_mx(
+                    out=hc[:, g, 0:n].bitcast(FP8X4),
+                    scales=hs[:, g, 0:n],
+                    in_=ghs[(s, g)][:, 0 : 4 * n],
+                )
+
+        def stage1(s):
+            c, t, h0, nh = units[s]
+            n = HALF * nh
+            hc, hs = hcs[s]
+            h2t = h2p.tile([P, 4, CH], BF16, name="h2t", tag="h2t")
+            h2ts[s] = h2t
+            for m in range(4):
+                ps = ps_s1.tile([P, CH], F32, name="ps1", tag="s1")
+                for g in range(2):
+                    nc.tensor.matmul_mx(
+                        out=ps[:, 0:n],
+                        lhsT=w2c[t][:, g, m * P : (m + 1) * P].bitcast(FP8X4),
+                        lhsT_scale=w2s[t][:, g, m * P : (m + 1) * P],
+                        rhs=hc[:, g, 0:n].bitcast(FP8X4),
+                        rhs_scale=hs[:, g, 0:n],
+                        start=(g == 0),
+                        stop=(g == 1),
+                    )
+                nc.scalar.activation(
+                    out=h2t[:, m, 0:n],
+                    in_=ps[:, 0:n],
+                    func=ACT.Relu,
+                    bias=bias2[:, 4 * t + m : 4 * t + m + 1],
+                    scale=1.0,
+                )
+
+        def regroup(s):
+            n = HALF * units[s][3]
             g2 = h2p.tile([P, 4 * CH], BF16, name="g2", tag="g2", align_bytes=64)
             nc.vector.tensor_copy(
-                out=g2[:].rearrange("p (c i t) -> p c t i", i=4, t=4),
-                in_=h2ts[r][:].rearrange("p t (c i) -> p c t i", i=4),
+                out=g2[:, 0 : 4 * n].rearrange("p (c i t) -> p c t i", i=4, t=4),
+                in_=h2ts[s][:, :, 0:n].rearrange("p t (c i) -> p c t i", i=4),
             )
-            g2s[r] = g2
+            g2s[s] = g2
 
-        def quant_h2(r):
-            h2c = h2cp.tile([P, CH], U32, name="h2c", tag="h2c", align_bytes=64)
-            h2s = h2cp.tile([P, CH], U8, name="h2s", tag="h2s", align_bytes=64)
-            nc.vector.quantize_mx(out=h2c[:].bitcast(FP8X4), scales=h2s[:], in_=g2s[r][:])
-            h2cs[r] = (h2c, h2s)
+        def quant_h2(s):
+            c, t, h0, nh = units[s]
+            n = HALF * nh
+            if h0 == 0:
+                h2c = h2cp.tile([P, CH], U32, name="h2c", tag="h2c", align_bytes=64)
+                h2s = h2cp.tile([P, CH], U8, name="h2s", tag="h2s", align_bytes=64)
+                h2cs[(c, t)] = (h2c, h2s)
+            h2c, h2s = h2cs[(c, t)]
+            lo = HALF * h0
+            nc.vector.quantize_mx(
+                out=h2c[:, lo : lo + n].bitcast(FP8X4),
+                scales=h2s[:, lo : lo + n],
+                in_=g2s[s][:, 0 : 4 * n],
+            )
 
-        def stage2(c, hf):
-            po = ps_s2.tile([P, 2, D_OUT], F32, name="po", tag="s2")
+        def stage2(c, hf, pool, tag):
+            po = pool.tile([P, 2, D_OUT], F32, name="po", tag=tag)
             for jj in range(2):
                 j = 2 * hf + jj
                 for t in range(T):
-                    h2c, h2s = h2cs[2 * c + t]
+                    h2c, h2s = h2cs[(c, t)]
                     nc.tensor.matmul_mx(
                         out=po[:, jj, :],
                         lhsT=h2c[:, j * P : (j + 1) * P].bitcast(FP8X4),
@@ -250,40 +295,56 @@ def tile_randomforestmlp_pa_t_kernel(tc, h1, W2, b2, W3, b3, out):
                 op0=ALU.mult,
                 op1=ALU.add,
             )
-            if hf == 1:
+            rows = out[c * CH : (c + 1) * CH, :].rearrange("(p j) o -> p j o", j=4)
+            if c == NCH - 1:
                 nc.sync.dma_start(
-                    out=out[c * CH : (c + 1) * CH, :].rearrange("(p j) o -> p j o", j=4),
-                    in_=osb[c][:],
+                    out=rows[:, 2 * hf : 2 * hf + 2, :], in_=osb[c][:, 2 * hf : 2 * hf + 2, :]
                 )
+            elif hf == 1:
+                nc.sync.dma_start(out=rows, in_=osb[c][:])
 
         prep_w2(0)
-        pending = None
-        for s in range(R + 5):
-            if s + AHEAD < R:
-                load_x(s + AHEAD)
-            r1, r2, a = s - 1, s - 2, s - 3
-            if s < R:
+        due = []
+        taken = 0
+        pending = []
+        for s in range(n_units + 4):
+            if s + AHEAD < len(rounds):
+                load_x(s + AHEAD, 1)
+            s1, s2 = s - 1, s - 2
+            if s < n_units:
                 transposes(s)
-            if 0 <= r2 < R:
-                regroup(r2)
-            if pending is not None:
-                exit_o(pending[0], pending[1])
-                pending = None
-            if 0 <= r2 < R:
-                quant_h2(r2)
-            if s < R:
-                for i in range(4):
-                    exit_t(s, i)
-            if 0 <= r1 < R:
-                for m in range(4):
-                    stage1(r1, m)
-            if s < R:
-                quant_h1(s, 0)
-                quant_h1(s, 1)
             if s == 0:
+                bias_matmuls()
+                bias_copies()
+            if 0 <= s2 < n_units:
+                regroup(s2)
+            if pending:
+                exit_o(pending[0][0], pending[0][1])
+            if 0 <= s2 < n_units:
+                quant_h2(s2)
+                c, t, h0, nh = units[s2]
+                if t == T - 1:
+                    for h in range(h0, h0 + nh):
+                        due.append((c, h))
+            for c, hf in pending[1:]:
+                exit_o(c, hf)
+            pending = []
+            if s < n_units:
+                exits_t(s)
+            if 0 <= s1 < n_units:
+                stage1(s1)
+            if s < n_units:
+                quant_h1(s)
+            if s == 2:
                 prep_w2(1)
-            if s == 1:
+            if s == 3:
                 prep_w3()
-            if 0 <= a < R:
-                stage2(a // 2, a % 2)
-                pending = (a // 2, a % 2)
+            tail = s >= n_units - 1
+            while taken < len(due) and (tail or not pending):
+                c, hf = due[taken]
+                taken += 1
+                if tail:
+                    stage2(c, hf, ps_tr, "tr")
+                else:
+                    stage2(c, hf, ps_s2, "s2")
+                pending.append((c, hf))

@@ -14,7 +14,6 @@ ALU = mybir.AluOpType
 T, B, D_H, D_K, D_OUT = 2, 4096, 1024, 512, 256
 P = 128
 CH = 512
-HALF = 256
 NCH = B // CH
 FLOPS = 2 * T * B * D_H * D_K + 2 * T * B * D_K * D_OUT
 
@@ -28,25 +27,24 @@ def tile_randomforestmlp_pa_t_kernel(tc, h1, W2, b2, W3, b3, out):
     rounds = [(2 * q + i, t) for q in range(NCH // 2) for t in range(T) for i in range(2)]
     units = []
     for r, (c, t) in enumerate(rounds):
-        if r == 0 or r == len(rounds) - 1:
-            units.append((c, t, 0, 1))
-            units.append((c, t, 1, 1))
+        if r == 0:
+            units.extend([(c, t, 0, 2), (c, t, 2, 2)])
+        elif r == len(rounds) - 1:
+            units.extend([(c, t, 0, 2), (c, t, 2, 1), (c, t, 3, 1)])
         else:
-            units.append((c, t, 0, 2))
+            units.append((c, t, 0, 4))
     n_units = len(units)
 
     with ExitStack() as ctx:
         const = ctx.enter_context(tc.tile_pool(name="const", bufs=1))
         xin = ctx.enter_context(tc.tile_pool(name="xin", bufs=NX))
         wst = ctx.enter_context(tc.tile_pool(name="wst", bufs=2))
-        ghp = ctx.enter_context(tc.tile_pool(name="ghp", bufs=4))
-        hcp = ctx.enter_context(tc.tile_pool(name="hcp", bufs=3))
-        h2p = ctx.enter_context(tc.tile_pool(name="h2p", bufs=2))
+        ghp = ctx.enter_context(tc.tile_pool(name="ghp", bufs=6))
+        hcp = ctx.enter_context(tc.tile_pool(name="hcp", bufs=4))
+        h2p = ctx.enter_context(tc.tile_pool(name="h2p", bufs=3))
         h2cp = ctx.enter_context(tc.tile_pool(name="h2cp", bufs=6))
         outp = ctx.enter_context(tc.tile_pool(name="outp", bufs=3))
-        ps_tr = ctx.enter_context(tc.psum_pool(name="ps_tr", bufs=4))
-        ps_s1 = ctx.enter_context(tc.psum_pool(name="ps_s1", bufs=3))
-        ps_s2 = ctx.enter_context(tc.psum_pool(name="ps_s2", bufs=1))
+        psum = ctx.enter_context(tc.psum_pool(name="psum", bufs=8))
         ctx.enter_context(tc.manual_schedule())
 
         xs = {}
@@ -114,7 +112,7 @@ def tile_randomforestmlp_pa_t_kernel(tc, h1, W2, b2, W3, b3, out):
         pbias = {}
 
         def bias_matmuls():
-            pb = ps_s2.tile([P, 512], F32, name="pb", tag="s2")
+            pb = psum.tile([P, 512], F32, name="pb", tag="bank")
             nc.tensor.matmul(
                 out=pb[:, 0:D_OUT], lhsT=halves[:], rhs=b3rows[:], start=True, stop=True
             )
@@ -175,37 +173,39 @@ def tile_randomforestmlp_pa_t_kernel(tc, h1, W2, b2, W3, b3, out):
         osb = {}
 
         def transposes(s):
-            c, t, h0, nh = units[s]
+            c, t, j0, nj = units[s]
             xw = xs[(c, t)][:].bitcast(F32)
             for g in range(2):
-                for h in range(h0, h0 + nh):
-                    bank = ps_tr.tile([P, 2, HALF], F32, name="trb", tag="tr")
+                for jb in range(0, nj, 2):
+                    w = min(2, nj - jb)
+                    bank = psum.tile([P, 2, 2 * P], F32, name="trb", tag="bank")
                     for u in range(2):
-                        for jj in range(2):
-                            col = (2 * h + jj) * 512 + g * 256 + u * 128
+                        for jj in range(w):
+                            col = (j0 + jb + jj) * 512 + g * 256 + u * 128
                             nc.tensor.transpose(
                                 out=bank[:, u, jj * P : (jj + 1) * P],
                                 in_=xw[:, col : col + P],
                                 identity=ident[:],
                             )
-                    trb[(s, g, h)] = bank
+                    trb[(s, g, jb)] = bank
 
         def exits_t(s):
-            c, t, h0, nh = units[s]
+            c, t, j0, nj = units[s]
             for g in range(2):
                 gh = ghp.tile([P, 4 * CH], BF16, name="gh", tag="gh", align_bytes=64)
                 ghs[(s, g)] = gh
                 words = gh[:].bitcast(F32).rearrange("p (n u) -> p n u", u=2)
-                for i in range(nh):
-                    dst = words[:, HALF * i : HALF * (i + 1), :]
-                    src = trb[(s, g, h0 + i)][:].rearrange("p u n -> p n u")
-                    if nh == 2 and s >= V_FROM and g == 1 and i == 1:
+                for jb in range(0, nj, 2):
+                    w = min(2, nj - jb)
+                    dst = words[:, P * jb : P * (jb + w), :]
+                    src = trb[(s, g, jb)][:, :, 0 : P * w].rearrange("p u n -> p n u")
+                    if nj == 4 and s >= V_FROM and s % 2 == 1 and g == 1 and jb == 2:
                         nc.vector.tensor_copy(out=dst, in_=src)
                     else:
                         nc.scalar.copy(out=dst, in_=src)
 
         def quant_h1(s):
-            n = HALF * units[s][3]
+            n = P * units[s][3]
             hc = hcp.tile([P, 2, CH], U32, name="hc", tag="hc", align_bytes=64)
             hs = hcp.tile([P, 2, CH], U8, name="hs", tag="hs", align_bytes=64)
             hcs[s] = (hc, hs)
@@ -217,13 +217,13 @@ def tile_randomforestmlp_pa_t_kernel(tc, h1, W2, b2, W3, b3, out):
                 )
 
         def stage1(s):
-            c, t, h0, nh = units[s]
-            n = HALF * nh
+            c, t, j0, nj = units[s]
+            n = P * nj
             hc, hs = hcs[s]
             h2t = h2p.tile([P, 4, CH], BF16, name="h2t", tag="h2t")
             h2ts[s] = h2t
             for m in range(4):
-                ps = ps_s1.tile([P, CH], F32, name="ps1", tag="s1")
+                ps = psum.tile([P, CH], F32, name="ps1", tag="bank")
                 for g in range(2):
                     nc.tensor.matmul_mx(
                         out=ps[:, 0:n],
@@ -243,7 +243,7 @@ def tile_randomforestmlp_pa_t_kernel(tc, h1, W2, b2, W3, b3, out):
                 )
 
         def regroup(s):
-            n = HALF * units[s][3]
+            n = P * units[s][3]
             g2 = h2p.tile([P, 4 * CH], BF16, name="g2", tag="g2", align_bytes=64)
             nc.vector.tensor_copy(
                 out=g2[:, 0 : 4 * n].rearrange("p (c i t) -> p c t i", i=4, t=4),
@@ -252,24 +252,22 @@ def tile_randomforestmlp_pa_t_kernel(tc, h1, W2, b2, W3, b3, out):
             g2s[s] = g2
 
         def quant_h2(s):
-            c, t, h0, nh = units[s]
-            n = HALF * nh
-            if h0 == 0:
+            c, t, j0, nj = units[s]
+            if j0 == 0:
                 h2c = h2cp.tile([P, CH], U32, name="h2c", tag="h2c", align_bytes=64)
                 h2s = h2cp.tile([P, CH], U8, name="h2s", tag="h2s", align_bytes=64)
                 h2cs[(c, t)] = (h2c, h2s)
             h2c, h2s = h2cs[(c, t)]
-            lo = HALF * h0
             nc.vector.quantize_mx(
-                out=h2c[:, lo : lo + n].bitcast(FP8X4),
-                scales=h2s[:, lo : lo + n],
-                in_=g2s[s][:, 0 : 4 * n],
+                out=h2c[:, P * j0 : P * (j0 + nj)].bitcast(FP8X4),
+                scales=h2s[:, P * j0 : P * (j0 + nj)],
+                in_=g2s[s][:, 0 : 4 * P * nj],
             )
 
-        def stage2(c, hf, pool, tag):
-            po = pool.tile([P, 2, D_OUT], F32, name="po", tag=tag)
-            for jj in range(2):
-                j = 2 * hf + jj
+        def stage2(c, j0, w):
+            po = psum.tile([P, 2, D_OUT], F32, name="po", tag="bank")
+            for jj in range(w):
+                j = j0 + jj
                 for t in range(T):
                     h2c, h2s = h2cs[(c, t)]
                     nc.tensor.matmul_mx(
@@ -281,26 +279,24 @@ def tile_randomforestmlp_pa_t_kernel(tc, h1, W2, b2, W3, b3, out):
                         start=(t == 0),
                         stop=(t == T - 1),
                     )
-            pos[(c, hf)] = po
+            pos[(c, j0)] = po
 
-        def exit_o(c, hf):
-            if hf == 0:
+        def exit_o(c, j0, w):
+            if j0 == 0:
                 o = outp.tile([P, 4, D_OUT], F32, name="o", tag="o")
                 osb[c] = o
             nc.vector.scalar_tensor_tensor(
-                out=osb[c][:, 2 * hf : 2 * hf + 2, :],
-                in0=pos[(c, hf)][:],
+                out=osb[c][:, j0 : j0 + w, :],
+                in0=pos[(c, j0)][:, 0:w, :],
                 scalar=0.5,
-                in1=b3bc[:],
+                in1=b3bc[:, 0:w, :],
                 op0=ALU.mult,
                 op1=ALU.add,
             )
             rows = out[c * CH : (c + 1) * CH, :].rearrange("(p j) o -> p j o", j=4)
             if c == NCH - 1:
-                nc.sync.dma_start(
-                    out=rows[:, 2 * hf : 2 * hf + 2, :], in_=osb[c][:, 2 * hf : 2 * hf + 2, :]
-                )
-            elif hf == 1:
+                nc.sync.dma_start(out=rows[:, j0 : j0 + w, :], in_=osb[c][:, j0 : j0 + w, :])
+            elif j0 + w == 4:
                 nc.sync.dma_start(out=rows, in_=osb[c][:])
 
         prep_w2(0)
@@ -311,6 +307,7 @@ def tile_randomforestmlp_pa_t_kernel(tc, h1, W2, b2, W3, b3, out):
             if s + AHEAD < len(rounds):
                 load_x(s + AHEAD, 1)
             s1, s2 = s - 1, s - 2
+            tail = s >= n_units - 1
             if s < n_units:
                 transposes(s)
             if s == 0:
@@ -318,16 +315,17 @@ def tile_randomforestmlp_pa_t_kernel(tc, h1, W2, b2, W3, b3, out):
                 bias_copies()
             if 0 <= s2 < n_units:
                 regroup(s2)
-            if pending:
-                exit_o(pending[0][0], pending[0][1])
+            if pending and not tail:
+                exit_o(pending[0][0], pending[0][1], pending[0][2])
+                pending = pending[1:]
             if 0 <= s2 < n_units:
                 quant_h2(s2)
-                c, t, h0, nh = units[s2]
+                c, t, j0, nj = units[s2]
                 if t == T - 1:
-                    for h in range(h0, h0 + nh):
-                        due.append((c, h))
-            for c, hf in pending[1:]:
-                exit_o(c, hf)
+                    for jb in range(0, nj, 2):
+                        due.append((c, j0 + jb, min(2, nj - jb)))
+            for c, j0, w in pending:
+                exit_o(c, j0, w)
             pending = []
             if s < n_units:
                 exits_t(s)
@@ -339,12 +337,8 @@ def tile_randomforestmlp_pa_t_kernel(tc, h1, W2, b2, W3, b3, out):
                 prep_w2(1)
             if s == 3:
                 prep_w3()
-            tail = s >= n_units - 1
             while taken < len(due) and (tail or not pending):
-                c, hf = due[taken]
+                c, j0, w = due[taken]
                 taken += 1
-                if tail:
-                    stage2(c, hf, ps_tr, "tr")
-                else:
-                    stage2(c, hf, ps_s2, "s2")
-                pending.append((c, hf))
+                stage2(c, j0, w)
+                pending.append((c, j0, w))

@@ -25,15 +25,20 @@ V_FROM = 5
 def tile_randomforestmlp_pa_t_kernel(tc, h1, W2, b2, W3, b3, out):
     nc = tc.nc
     rounds = [(2 * q + i, t) for q in range(NCH // 2) for t in range(T) for i in range(2)]
-    units = []
+    fronts = []
+    backs = []
     for r, (c, t) in enumerate(rounds):
         if r == 0:
-            units.extend([(c, t, 0, 2), (c, t, 2, 2)])
+            fronts.extend([(c, t, 0, 2), (c, t, 2, 2)])
+            backs.extend([(c, t, 0, 2), (c, t, 2, 2)])
         elif r == len(rounds) - 1:
-            units.extend([(c, t, 0, 2), (c, t, 2, 1), (c, t, 3, 1)])
+            fronts.append((c, t, 0, 4))
+            backs.extend([(c, t, 0, 2), (c, t, 2, 1), (c, t, 3, 1)])
         else:
-            units.append((c, t, 0, 4))
-    n_units = len(units)
+            fronts.append((c, t, 0, 4))
+            backs.append((c, t, 0, 4))
+    n_fronts = len(fronts)
+    n_backs = len(backs)
 
     with ExitStack() as ctx:
         const = ctx.enter_context(tc.tile_pool(name="const", bufs=1))
@@ -45,7 +50,6 @@ def tile_randomforestmlp_pa_t_kernel(tc, h1, W2, b2, W3, b3, out):
         h2cp = ctx.enter_context(tc.tile_pool(name="h2cp", bufs=6))
         outp = ctx.enter_context(tc.tile_pool(name="outp", bufs=3))
         psum = ctx.enter_context(tc.psum_pool(name="psum", bufs=8))
-        ctx.enter_context(tc.manual_schedule())
 
         xs = {}
 
@@ -88,10 +92,10 @@ def tile_randomforestmlp_pa_t_kernel(tc, h1, W2, b2, W3, b3, out):
         nc.vector.memset(b3rows[:], 0.0)
         halves = const.tile([P, P], BF16, name="halves")
         nc.vector.memset(halves[:], 0.5)
-        nc.sync.dma_start(out=b2rows[0:8, :], in_=b2.rearrange("t (m i) -> (t m) i", i=P))
-        nc.sync.dma_start(out=b3rows[0:2, :], in_=b3)
 
         load_w2(0)
+        nc.sync.dma_start(out=b2rows[0:8, :], in_=b2.rearrange("t (m i) -> (t m) i", i=P))
+        nc.sync.dma_start(out=b3rows[0:2, :], in_=b3)
         load_x(0, 2)
         load_x(1, 1)
         load_x(2, 1)
@@ -173,7 +177,7 @@ def tile_randomforestmlp_pa_t_kernel(tc, h1, W2, b2, W3, b3, out):
         osb = {}
 
         def transposes(s):
-            c, t, j0, nj = units[s]
+            c, t, j0, nj = fronts[s]
             xw = xs[(c, t)][:].bitcast(F32)
             for g in range(2):
                 for jb in range(0, nj, 2):
@@ -190,7 +194,7 @@ def tile_randomforestmlp_pa_t_kernel(tc, h1, W2, b2, W3, b3, out):
                     trb[(s, g, jb)] = bank
 
         def exits_t(s):
-            c, t, j0, nj = units[s]
+            c, t, j0, nj = fronts[s]
             for g in range(2):
                 gh = ghp.tile([P, 4 * CH], BF16, name="gh", tag="gh", align_bytes=64)
                 ghs[(s, g)] = gh
@@ -205,10 +209,12 @@ def tile_randomforestmlp_pa_t_kernel(tc, h1, W2, b2, W3, b3, out):
                         nc.scalar.copy(out=dst, in_=src)
 
         def quant_h1(s):
-            n = P * units[s][3]
+            c, t, j0, nj = fronts[s]
+            n = P * nj
             hc = hcp.tile([P, 2, CH], U32, name="hc", tag="hc", align_bytes=64)
             hs = hcp.tile([P, 2, CH], U8, name="hs", tag="hs", align_bytes=64)
-            hcs[s] = (hc, hs)
+            for j in range(j0, j0 + nj):
+                hcs[(c, t, j)] = (hc, hs, P * (j - j0))
             for g in range(2):
                 nc.vector.quantize_mx(
                     out=hc[:, g, 0:n].bitcast(FP8X4),
@@ -217,9 +223,9 @@ def tile_randomforestmlp_pa_t_kernel(tc, h1, W2, b2, W3, b3, out):
                 )
 
         def stage1(s):
-            c, t, j0, nj = units[s]
+            c, t, j0, nj = backs[s]
             n = P * nj
-            hc, hs = hcs[s]
+            hc, hs, lo = hcs[(c, t, j0)]
             h2t = h2p.tile([P, 4, CH], BF16, name="h2t", tag="h2t")
             h2ts[s] = h2t
             for m in range(4):
@@ -229,8 +235,8 @@ def tile_randomforestmlp_pa_t_kernel(tc, h1, W2, b2, W3, b3, out):
                         out=ps[:, 0:n],
                         lhsT=w2c[t][:, g, m * P : (m + 1) * P].bitcast(FP8X4),
                         lhsT_scale=w2s[t][:, g, m * P : (m + 1) * P],
-                        rhs=hc[:, g, 0:n].bitcast(FP8X4),
-                        rhs_scale=hs[:, g, 0:n],
+                        rhs=hc[:, g, lo : lo + n].bitcast(FP8X4),
+                        rhs_scale=hs[:, g, lo : lo + n],
                         start=(g == 0),
                         stop=(g == 1),
                     )
@@ -243,7 +249,7 @@ def tile_randomforestmlp_pa_t_kernel(tc, h1, W2, b2, W3, b3, out):
                 )
 
         def regroup(s):
-            n = P * units[s][3]
+            n = P * backs[s][3]
             g2 = h2p.tile([P, 4 * CH], BF16, name="g2", tag="g2", align_bytes=64)
             nc.vector.tensor_copy(
                 out=g2[:, 0 : 4 * n].rearrange("p (c i t) -> p c t i", i=4, t=4),
@@ -252,7 +258,7 @@ def tile_randomforestmlp_pa_t_kernel(tc, h1, W2, b2, W3, b3, out):
             g2s[s] = g2
 
         def quant_h2(s):
-            c, t, j0, nj = units[s]
+            c, t, j0, nj = backs[s]
             if j0 == 0:
                 h2c = h2cp.tile([P, CH], U32, name="h2c", tag="h2c", align_bytes=64)
                 h2s = h2cp.tile([P, CH], U8, name="h2s", tag="h2s", align_bytes=64)
@@ -303,42 +309,42 @@ def tile_randomforestmlp_pa_t_kernel(tc, h1, W2, b2, W3, b3, out):
         due = []
         taken = 0
         pending = []
-        for s in range(n_units + 4):
+        for s in range(n_backs + 5):
             if s + AHEAD < len(rounds):
                 load_x(s + AHEAD, 1)
             s1, s2 = s - 1, s - 2
-            tail = s >= n_units - 1
-            if s < n_units:
+            tail = s >= n_fronts
+            if s < n_fronts:
                 transposes(s)
             if s == 0:
                 bias_matmuls()
                 bias_copies()
-            if 0 <= s2 < n_units:
+            if 0 <= s2 < n_backs:
                 regroup(s2)
             if pending and not tail:
                 exit_o(pending[0][0], pending[0][1], pending[0][2])
                 pending = pending[1:]
-            if 0 <= s2 < n_units:
+            if 0 <= s2 < n_backs:
                 quant_h2(s2)
-                c, t, j0, nj = units[s2]
+                c, t, j0, nj = backs[s2]
                 if t == T - 1:
                     for jb in range(0, nj, 2):
-                        due.append((c, j0 + jb, min(2, nj - jb)))
+                        due.append((c, j0 + jb, min(2, nj - jb), s))
             for c, j0, w in pending:
                 exit_o(c, j0, w)
             pending = []
-            if s < n_units:
+            if s < n_fronts:
                 exits_t(s)
-            if 0 <= s1 < n_units:
+            if 0 <= s1 < n_backs:
                 stage1(s1)
-            if s < n_units:
+            if s < n_fronts:
                 quant_h1(s)
             if s == 2:
                 prep_w2(1)
             if s == 3:
                 prep_w3()
-            while taken < len(due) and (tail or not pending):
-                c, j0, w = due[taken]
+            while taken < len(due) and due[taken][3] < s and (tail or not pending):
+                c, j0, w = due[taken][0:3]
                 taken += 1
                 stage2(c, j0, w)
                 pending.append((c, j0, w))

@@ -55,7 +55,7 @@ def tile_randomforestmlp_pa_t_kernel(tc, h1, W2, b2, W3, b3, out):
 
         def load_x(r, pieces):
             c, t = rounds[r]
-            x = xin.tile([P, 4 * D_H], BF16, name="x", tag="x")
+            x = xin.tile([P, 4 * D_H], BF16, name="x", tag="x", align_bytes=256)
             rows = h1[t, c * CH : (c + 1) * CH, :].rearrange("(p j) k -> p j k", j=4)
             step = 4 // pieces
             for i in range(pieces):
@@ -136,15 +136,15 @@ def tile_randomforestmlp_pa_t_kernel(tc, h1, W2, b2, W3, b3, out):
         w3c = {}
         w3s = {}
         for t in range(T):
-            w2c[t] = const.tile([P, 2, D_K], U32, name="w2c%d" % t, align_bytes=64)
-            w2s[t] = const.tile([P, 2, D_K], U8, name="w2s%d" % t, align_bytes=64)
-            w3c[t] = const.tile([P, D_OUT], U32, name="w3c%d" % t, align_bytes=64)
-            w3s[t] = const.tile([P, D_OUT], U8, name="w3s%d" % t, align_bytes=64)
+            w2c[t] = const.tile([P, 2, D_K], U32, name="w2c%d" % t, align_bytes=256)
+            w2s[t] = const.tile([P, 2, D_K], U8, name="w2s%d" % t, align_bytes=256)
+            w3c[t] = const.tile([P, D_OUT], U32, name="w3c%d" % t, align_bytes=256)
+            w3s[t] = const.tile([P, D_OUT], U8, name="w3s%d" % t, align_bytes=256)
 
         def prep_w2(t):
             grp = {}
             for g in range(2):
-                wg = wst.tile([P, 4 * D_K], BF16, name="wg", tag="wg", align_bytes=64)
+                wg = wst.tile([P, 4 * D_K], BF16, name="wg", tag="wg", align_bytes=256)
                 nc.vector.tensor_copy(
                     out=wg[:].rearrange("p (c i t) -> p c t i", i=4, t=4),
                     in_=w2raw[t][:, 4 * g : 4 * g + 4, :].rearrange("p t (c i) -> p c t i", i=4),
@@ -158,7 +158,7 @@ def tile_randomforestmlp_pa_t_kernel(tc, h1, W2, b2, W3, b3, out):
         def prep_w3():
             grp = {}
             for t in range(T):
-                wg = wst.tile([P, 4 * D_OUT], BF16, name="wg3", tag="wg", align_bytes=64)
+                wg = wst.tile([P, 4 * D_OUT], BF16, name="wg3", tag="wg", align_bytes=256)
                 nc.vector.tensor_copy(
                     out=wg[:].rearrange("p (c i t) -> p c t i", i=4, t=4),
                     in_=w3raw[t][:].rearrange("p t (c i) -> p c t i", i=4),
@@ -196,7 +196,7 @@ def tile_randomforestmlp_pa_t_kernel(tc, h1, W2, b2, W3, b3, out):
         def exits_t(s):
             c, t, j0, nj = fronts[s]
             for g in range(2):
-                gh = ghp.tile([P, 4 * CH], BF16, name="gh", tag="gh", align_bytes=64)
+                gh = ghp.tile([P, 4 * CH], BF16, name="gh", tag="gh", align_bytes=256)
                 ghs[(s, g)] = gh
                 words = gh[:].bitcast(F32).rearrange("p (n u) -> p n u", u=2)
                 for jb in range(0, nj, 2):
@@ -211,8 +211,8 @@ def tile_randomforestmlp_pa_t_kernel(tc, h1, W2, b2, W3, b3, out):
         def quant_h1(s):
             c, t, j0, nj = fronts[s]
             n = P * nj
-            hc = hcp.tile([P, 2, CH], U32, name="hc", tag="hc", align_bytes=64)
-            hs = hcp.tile([P, 2, CH], U8, name="hs", tag="hs", align_bytes=64)
+            hc = hcp.tile([P, 2, CH], U32, name="hc", tag="hc", align_bytes=256)
+            hs = hcp.tile([P, 2, CH], U8, name="hs", tag="hs", align_bytes=256)
             for j in range(j0, j0 + nj):
                 hcs[(c, t, j)] = (hc, hs, P * (j - j0))
             for g in range(2):
@@ -226,7 +226,7 @@ def tile_randomforestmlp_pa_t_kernel(tc, h1, W2, b2, W3, b3, out):
             c, t, j0, nj = backs[s]
             n = P * nj
             hc, hs, lo = hcs[(c, t, j0)]
-            h2t = h2p.tile([P, 4, CH], BF16, name="h2t", tag="h2t")
+            h2t = h2p.tile([P, 4, CH], BF16, name="h2t", tag="h2t", align_bytes=256)
             h2ts[s] = h2t
             for m in range(4):
                 ps = psum.tile([P, CH], F32, name="ps1", tag="bank")
@@ -250,7 +250,7 @@ def tile_randomforestmlp_pa_t_kernel(tc, h1, W2, b2, W3, b3, out):
 
         def regroup(s):
             n = P * backs[s][3]
-            g2 = h2p.tile([P, 4 * CH], BF16, name="g2", tag="g2", align_bytes=64)
+            g2 = h2p.tile([P, 4 * CH], BF16, name="g2", tag="g2", align_bytes=256)
             nc.vector.tensor_copy(
                 out=g2[:, 0 : 4 * n].rearrange("p (c i t) -> p c t i", i=4, t=4),
                 in_=h2ts[s][:, :, 0:n].rearrange("p t (c i) -> p c t i", i=4),
@@ -260,8 +260,8 @@ def tile_randomforestmlp_pa_t_kernel(tc, h1, W2, b2, W3, b3, out):
         def quant_h2(s):
             c, t, j0, nj = backs[s]
             if j0 == 0:
-                h2c = h2cp.tile([P, CH], U32, name="h2c", tag="h2c", align_bytes=64)
-                h2s = h2cp.tile([P, CH], U8, name="h2s", tag="h2s", align_bytes=64)
+                h2c = h2cp.tile([P, CH], U32, name="h2c", tag="h2c", align_bytes=256)
+                h2s = h2cp.tile([P, CH], U8, name="h2s", tag="h2s", align_bytes=256)
                 h2cs[(c, t)] = (h2c, h2s)
             h2c, h2s = h2cs[(c, t)]
             nc.vector.quantize_mx(

@@ -248,13 +248,19 @@ def tile_randomforestmlp_pa_t_kernel(tc, h1, W2, b2, W3, b3, out):
                     scale=1.0,
                 )
 
+        def parts(n):
+            if n == P:
+                return [(0, n)]
+            return [(0, n // 2), (n // 2, n)]
+
         def regroup(s):
             n = P * backs[s][3]
             g2 = h2p.tile([P, 4 * CH], BF16, name="g2", tag="g2", align_bytes=256)
-            nc.vector.tensor_copy(
-                out=g2[:, 0 : 4 * n].rearrange("p (c i t) -> p c t i", i=4, t=4),
-                in_=h2ts[s][:, :, 0:n].rearrange("p t (c i) -> p c t i", i=4),
-            )
+            for lo, hi in parts(n):
+                nc.vector.tensor_copy(
+                    out=g2[:, 4 * lo : 4 * hi].rearrange("p (c i t) -> p c t i", i=4, t=4),
+                    in_=h2ts[s][:, :, lo:hi].rearrange("p t (c i) -> p c t i", i=4),
+                )
             g2s[s] = g2
 
         def quant_h2(s):
@@ -264,11 +270,12 @@ def tile_randomforestmlp_pa_t_kernel(tc, h1, W2, b2, W3, b3, out):
                 h2s = h2cp.tile([P, CH], U8, name="h2s", tag="h2s", align_bytes=256)
                 h2cs[(c, t)] = (h2c, h2s)
             h2c, h2s = h2cs[(c, t)]
-            nc.vector.quantize_mx(
-                out=h2c[:, P * j0 : P * (j0 + nj)].bitcast(FP8X4),
-                scales=h2s[:, P * j0 : P * (j0 + nj)],
-                in_=g2s[s][:, 0 : 4 * P * nj],
-            )
+            for lo, hi in parts(P * nj):
+                nc.vector.quantize_mx(
+                    out=h2c[:, P * j0 + lo : P * j0 + hi].bitcast(FP8X4),
+                    scales=h2s[:, P * j0 + lo : P * j0 + hi],
+                    in_=g2s[s][:, 4 * lo : 4 * hi],
+                )
 
         def stage2(c, j0, w):
             po = psum.tile([P, 2, D_OUT], F32, name="po", tag="bank")

@@ -19,7 +19,8 @@ FLOPS = 2 * T * B * D_H * D_K + 2 * T * B * D_K * D_OUT
 
 NX = 8
 AHEAD = 6
-V_FROM = 5
+V_FROM = 7
+HEAD_STEPS = 5
 
 
 def tile_randomforestmlp_pa_t_kernel(tc, h1, W2, b2, W3, b3, out):
@@ -53,33 +54,28 @@ def tile_randomforestmlp_pa_t_kernel(tc, h1, W2, b2, W3, b3, out):
 
         xs = {}
 
-        def load_x(r, pieces):
+        def load_x(r, j0=0, nj=4):
             c, t = rounds[r]
-            x = xin.tile([P, 4 * D_H], BF16, name="x", tag="x", align_bytes=256)
+            if j0 == 0:
+                xs[(c, t)] = xin.tile([P, 4 * D_H], BF16, name="x", tag="x", align_bytes=256)
             rows = h1[t, c * CH : (c + 1) * CH, :].rearrange("(p j) k -> p j k", j=4)
-            step = 4 // pieces
-            for i in range(pieces):
-                nc.sync.dma_start(
-                    out=x[:, i * step * D_H : (i + 1) * step * D_H].rearrange(
-                        "p (j k) -> p j k", j=step
-                    ),
-                    in_=rows[:, i * step : (i + 1) * step, :],
-                )
-            xs[(c, t)] = x
+            nc.sync.dma_start(
+                out=xs[(c, t)][:, j0 * D_H : (j0 + nj) * D_H].rearrange("p (j k) -> p j k", j=nj),
+                in_=rows[:, j0 : j0 + nj, :],
+            )
 
         w2raw = {}
         w3raw = {}
 
-        def load_w2(t):
-            w = const.tile([P, 8, D_K], BF16, name="w2raw%d" % t)
-            for g in range(2):
-                nc.sync.dma_start(
-                    out=w[:, 4 * g : 4 * g + 4, :].rearrange("p (u e) w -> p u e w", e=2),
-                    in_=W2[t, g * 512 : (g + 1) * 512, :].rearrange(
-                        "(u p e) w -> p u e w", u=2, p=P, e=2
-                    ),
-                )
-            w2raw[t] = w
+        def load_w2(t, g):
+            if g == 0:
+                w2raw[t] = const.tile([P, 8, D_K], BF16, name="w2raw%d" % t)
+            nc.sync.dma_start(
+                out=w2raw[t][:, 4 * g : 4 * g + 4, :].rearrange("p (u e) w -> p u e w", e=2),
+                in_=W2[t, g * 512 : (g + 1) * 512, :].rearrange(
+                    "(u p e) w -> p u e w", u=2, p=P, e=2
+                ),
+            )
 
         def load_w3(t):
             w = const.tile([P, 4, D_OUT], BF16, name="w3raw%d" % t)
@@ -93,23 +89,26 @@ def tile_randomforestmlp_pa_t_kernel(tc, h1, W2, b2, W3, b3, out):
         halves = const.tile([P, P], BF16, name="halves")
         nc.vector.memset(halves[:], 0.5)
 
-        load_w2(0)
+        load_w2(0, 0)
         nc.sync.dma_start(out=b2rows[0:8, :], in_=b2.rearrange("t (m i) -> (t m) i", i=P))
         nc.sync.dma_start(out=b3rows[0:2, :], in_=b3)
-        load_x(0, 2)
-        load_x(1, 1)
-        load_x(2, 1)
-        load_w2(1)
-        load_x(3, 1)
+        load_x(0, 0, 2)
+        load_w2(0, 1)
+        load_x(0, 2, 2)
+        load_x(1)
+        load_x(2)
+        load_w2(1, 0)
+        load_w2(1, 1)
+        load_x(3)
         load_w3(0)
         load_w3(1)
         for r in range(4, AHEAD):
-            load_x(r, 1)
+            load_x(r)
 
         ident = const.tile([P, P], F32, name="ident")
         make_identity(nc, ident[:])
         ident_bf = const.tile([P, 32], BF16, name="ident_bf")
-        nc.vector.tensor_copy(out=ident_bf[:], in_=ident[:, 0:32])
+        nc.gpsimd.tensor_copy(out=ident_bf[:], in_=ident[:, 0:32])
 
         bias2 = const.tile([P, 8], F32, name="bias2")
         b3bc = const.tile([P, 2, D_OUT], F32, name="b3bc")
@@ -127,9 +126,9 @@ def tile_randomforestmlp_pa_t_kernel(tc, h1, W2, b2, W3, b3, out):
 
         def bias_copies():
             pb = pbias[0]
-            nc.vector.tensor_copy(out=bias2[:], in_=pb[:, D_OUT : D_OUT + 8])
-            nc.vector.tensor_copy(out=b3bc[:, 0, :], in_=pb[:, 0:D_OUT])
-            nc.vector.tensor_copy(out=b3bc[:, 1, :], in_=pb[:, 0:D_OUT])
+            nc.scalar.copy(out=bias2[:], in_=pb[:, D_OUT : D_OUT + 8])
+            nc.scalar.copy(out=b3bc[:, 0, :], in_=pb[:, 0:D_OUT])
+            nc.scalar.copy(out=b3bc[:, 1, :], in_=pb[:, 0:D_OUT])
 
         w2c = {}
         w2s = {}
@@ -312,20 +311,24 @@ def tile_randomforestmlp_pa_t_kernel(tc, h1, W2, b2, W3, b3, out):
             elif j0 + w == 4:
                 nc.sync.dma_start(out=rows, in_=osb[c][:])
 
+        bias_matmuls()
+        bias_copies()
         prep_w2(0)
         due = []
-        taken = 0
-        pending = []
-        for s in range(n_backs + 5):
+        state = {"taken": 0, "pending": []}
+        def step(s):
+            taken = state["taken"]
+            pending = state["pending"]
             if s + AHEAD < len(rounds):
-                load_x(s + AHEAD, 1)
+                load_x(s + AHEAD)
             s1, s2 = s - 1, s - 2
             tail = s >= n_fronts
             if s < n_fronts:
                 transposes(s)
-            if s == 0:
-                bias_matmuls()
-                bias_copies()
+            first = s == 3
+            if first:
+                exits_t(s)
+                quant_h1(s)
             if 0 <= s2 < n_backs:
                 regroup(s2)
             if pending and not tail:
@@ -340,18 +343,26 @@ def tile_randomforestmlp_pa_t_kernel(tc, h1, W2, b2, W3, b3, out):
             for c, j0, w in pending:
                 exit_o(c, j0, w)
             pending = []
-            if s < n_fronts:
+            if s < n_fronts and not first:
                 exits_t(s)
             if 0 <= s1 < n_backs:
                 stage1(s1)
-            if s < n_fronts:
+            if s < n_fronts and not first:
                 quant_h1(s)
             if s == 2:
                 prep_w2(1)
-            if s == 3:
+            if s == 4:
                 prep_w3()
             while taken < len(due) and due[taken][3] < s and (tail or not pending):
                 c, j0, w = due[taken][0:3]
                 taken += 1
                 stage2(c, j0, w)
                 pending.append((c, j0, w))
+            state["taken"] = taken
+            state["pending"] = pending
+
+        with tc.manual_schedule(engines={mybir.EngineType.DVE}):
+            for s in range(HEAD_STEPS):
+                step(s)
+        for s in range(HEAD_STEPS, n_backs + 5):
+            step(s)

@@ -202,7 +202,7 @@ def tile_randomforestmlp_pa_t_kernel(tc, h1, W2, b2, W3, b3, out):
                     w = min(2, nj - jb)
                     dst = words[:, P * jb : P * (jb + w), :]
                     src = trb[(s, g, jb)][:, :, 0 : P * w].rearrange("p u n -> p n u")
-                    if nj == 4 and s >= V_FROM and s % 2 == 1 and g == 1 and jb == 2:
+                    if s in (7, 9, 11) and g == 1 and jb == 2:
                         nc.vector.tensor_copy(out=dst, in_=src)
                     else:
                         nc.scalar.copy(out=dst, in_=src)
@@ -255,8 +255,9 @@ def tile_randomforestmlp_pa_t_kernel(tc, h1, W2, b2, W3, b3, out):
         def regroup(s):
             n = P * backs[s][3]
             g2 = h2p.tile([P, 4 * CH], BF16, name="g2", tag="g2", align_bytes=256)
+            copy = nc.scalar.copy if s >= n_backs - 2 else nc.vector.tensor_copy
             for lo, hi in parts(n):
-                nc.vector.tensor_copy(
+                copy(
                     out=g2[:, 4 * lo : 4 * hi].rearrange("p (c i t) -> p c t i", i=4, t=4),
                     in_=h2ts[s][:, :, lo:hi].rearrange("p t (c i) -> p c t i", i=4),
                 )
@@ -306,7 +307,7 @@ def tile_randomforestmlp_pa_t_kernel(tc, h1, W2, b2, W3, b3, out):
                 op1=ALU.add,
             )
             rows = out[c * CH : (c + 1) * CH, :].rearrange("(p j) o -> p j o", j=4)
-            if c == NCH - 1:
+            if c >= NCH - 2:
                 nc.sync.dma_start(out=rows[:, j0 : j0 + w, :], in_=osb[c][:, j0 : j0 + w, :])
             elif j0 + w == 4:
                 nc.sync.dma_start(out=rows, in_=osb[c][:])
@@ -345,8 +346,11 @@ def tile_randomforestmlp_pa_t_kernel(tc, h1, W2, b2, W3, b3, out):
             pending = []
             if s < n_fronts and not first:
                 exits_t(s)
-            if 0 <= s1 < n_backs:
+            if 0 <= s1 < n_fronts - 1:
                 stage1(s1)
+            elif s1 == n_fronts - 1:
+                for b in range(s1, n_backs):
+                    stage1(b)
             if s < n_fronts and not first:
                 quant_h1(s)
             if s == 2:

@@ -96,8 +96,8 @@ def tile_randomforestmlp_pa_t_kernel(tc, h1, W2, b2, W3, b3, out):
         load_w2(0, 1)
         load_x(0, 2, 2)
         load_x(1)
-        load_x(2)
         load_w2(1, 0)
+        load_x(2)
         load_w2(1, 1)
         load_x(3)
         load_w3(0)
@@ -140,19 +140,20 @@ def tile_randomforestmlp_pa_t_kernel(tc, h1, W2, b2, W3, b3, out):
             w3c[t] = const.tile([P, D_OUT], U32, name="w3c%d" % t, align_bytes=256)
             w3s[t] = const.tile([P, D_OUT], U8, name="w3s%d" % t, align_bytes=256)
 
-        def prep_w2(t):
-            grp = {}
-            for g in range(2):
-                wg = wst.tile([P, 4 * D_K], BF16, name="wg", tag="wg", align_bytes=256)
-                nc.vector.tensor_copy(
-                    out=wg[:].rearrange("p (c i t) -> p c t i", i=4, t=4),
-                    in_=w2raw[t][:, 4 * g : 4 * g + 4, :].rearrange("p t (c i) -> p c t i", i=4),
-                )
-                grp[g] = wg
-            for g in range(2):
-                nc.vector.quantize_mx(
-                    out=w2c[t][:, g, :].bitcast(FP8X4), scales=w2s[t][:, g, :], in_=grp[g][:]
-                )
+        grp2 = {}
+
+        def regroup_w2(t, g):
+            wg = wst.tile([P, 4 * D_K], BF16, name="wg", tag="wg", align_bytes=256)
+            nc.vector.tensor_copy(
+                out=wg[:].rearrange("p (c i t) -> p c t i", i=4, t=4),
+                in_=w2raw[t][:, 4 * g : 4 * g + 4, :].rearrange("p t (c i) -> p c t i", i=4),
+            )
+            grp2[g] = wg
+
+        def quant_w2(t, g):
+            nc.vector.quantize_mx(
+                out=w2c[t][:, g, :].bitcast(FP8X4), scales=w2s[t][:, g, :], in_=grp2[g][:]
+            )
 
         def prep_w3():
             grp = {}
@@ -202,7 +203,7 @@ def tile_randomforestmlp_pa_t_kernel(tc, h1, W2, b2, W3, b3, out):
                     w = min(2, nj - jb)
                     dst = words[:, P * jb : P * (jb + w), :]
                     src = trb[(s, g, jb)][:, :, 0 : P * w].rearrange("p u n -> p n u")
-                    if s in (7, 9, 11) and g == 1 and jb == 2:
+                    if s in (7, 9, 11, 13) and g == 1 and jb == 2:
                         nc.vector.tensor_copy(out=dst, in_=src)
                     else:
                         nc.scalar.copy(out=dst, in_=src)
@@ -314,7 +315,10 @@ def tile_randomforestmlp_pa_t_kernel(tc, h1, W2, b2, W3, b3, out):
 
         bias_matmuls()
         bias_copies()
-        prep_w2(0)
+        regroup_w2(0, 0)
+        regroup_w2(0, 1)
+        quant_w2(0, 0)
+        quant_w2(0, 1)
         due = []
         state = {"taken": 0, "pending": []}
         def step(s):
@@ -326,6 +330,8 @@ def tile_randomforestmlp_pa_t_kernel(tc, h1, W2, b2, W3, b3, out):
             tail = s >= n_fronts
             if s < n_fronts:
                 transposes(s)
+            if s == 2:
+                regroup_w2(1, 0)
             first = s == 3
             if first:
                 exits_t(s)
@@ -354,7 +360,9 @@ def tile_randomforestmlp_pa_t_kernel(tc, h1, W2, b2, W3, b3, out):
             if s < n_fronts and not first:
                 quant_h1(s)
             if s == 2:
-                prep_w2(1)
+                regroup_w2(1, 1)
+                quant_w2(1, 0)
+                quant_w2(1, 1)
             if s == 4:
                 prep_w3()
             while taken < len(due) and due[taken][3] < s and (tail or not pending):

from contextlib import ExitStack

import concourse.mybir as mybir
from concourse.masks import make_identity

F32 = mybir.dt.float32
BF16 = mybir.dt.bfloat16
U32 = mybir.dt.uint32
U8 = mybir.dt.uint8
FP8X4 = mybir.dt.float8_e4m3fn_x4
ACT = mybir.ActivationFunctionType
ALU = mybir.AluOpType

T, B, D_H, D_K, D_OUT = 2, 4096, 1024, 512, 256
P = 128
CH = 512
NCH = B // CH
FLOPS = 2 * T * B * D_H * D_K + 2 * T * B * D_K * D_OUT

NX = 8
AHEAD = 6
V_FROM = 7
HEAD_STEPS = 5


def tile_randomforestmlp_pa_t_kernel(tc, h1, W2, b2, W3, b3, out):
    nc = tc.nc
    rounds = [(2 * q + i, t) for q in range(NCH // 2) for t in range(T) for i in range(2)]
    fronts = []
    backs = []
    for r, (c, t) in enumerate(rounds):
        if r == 0:
            fronts.extend([(c, t, 0, 2), (c, t, 2, 2)])
            backs.extend([(c, t, 0, 2), (c, t, 2, 2)])
        elif r == len(rounds) - 1:
            fronts.append((c, t, 0, 4))
            backs.extend([(c, t, 0, 2), (c, t, 2, 1), (c, t, 3, 1)])
        else:
            fronts.append((c, t, 0, 4))
            backs.append((c, t, 0, 4))
    n_fronts = len(fronts)
    n_backs = len(backs)

    with ExitStack() as ctx:
        const = ctx.enter_context(tc.tile_pool(name="const", bufs=1))
        xin = ctx.enter_context(tc.tile_pool(name="xin", bufs=NX))
        wst = ctx.enter_context(tc.tile_pool(name="wst", bufs=2))
        ghp = ctx.enter_context(tc.tile_pool(name="ghp", bufs=6))
        hcp = ctx.enter_context(tc.tile_pool(name="hcp", bufs=4))
        h2p = ctx.enter_context(tc.tile_pool(name="h2p", bufs=3))
        h2cp = ctx.enter_context(tc.tile_pool(name="h2cp", bufs=6))
        outp = ctx.enter_context(tc.tile_pool(name="outp", bufs=3))
        psum = ctx.enter_context(tc.psum_pool(name="psum", bufs=8))

        xs = {}

        def load_x(r, j0=0, nj=4):
            c, t = rounds[r]
            if j0 == 0:
                xs[(c, t)] = xin.tile([P, 4 * D_H], BF16, name="x", tag="x", align_bytes=256)
            rows = h1[t, c * CH : (c + 1) * CH, :].rearrange("(p j) k -> p j k", j=4)
            nc.sync.dma_start(
                out=xs[(c, t)][:, j0 * D_H : (j0 + nj) * D_H].rearrange("p (j k) -> p j k", j=nj),
                in_=rows[:, j0 : j0 + nj, :],
            )

        w2raw = {}
        w3raw = {}

        def load_w2(t, g):
            if g == 0:
                w2raw[t] = const.tile([P, 8, D_K], BF16, name="w2raw%d" % t)
            nc.sync.dma_start(
                out=w2raw[t][:, 4 * g : 4 * g + 4, :].rearrange("p (u e) w -> p u e w", e=2),
                in_=W2[t, g * 512 : (g + 1) * 512, :].rearrange(
                    "(u p e) w -> p u e w", u=2, p=P, e=2
                ),
            )

        def load_w3(t):
            w = const.tile([P, 4, D_OUT], BF16, name="w3raw%d" % t)
            nc.sync.dma_start(out=w[:], in_=W3[t].rearrange("(m p) o -> p m o", p=P))
            w3raw[t] = w

        b2rows = const.tile([P, P], BF16, name="b2rows")
        nc.vector.memset(b2rows[:], 0.0)
        b3rows = const.tile([P, D_OUT], BF16, name="b3rows")
        nc.vector.memset(b3rows[:], 0.0)
        halves = const.tile([P, P], BF16, name="halves")
        nc.vector.memset(halves[:], 0.5)

        load_w2(0, 0)
        nc.sync.dma_start(out=b2rows[0:8, :], in_=b2.rearrange("t (m i) -> (t m) i", i=P))
        nc.sync.dma_start(out=b3rows[0:2, :], in_=b3)
        load_x(0, 0, 2)
        load_w2(0, 1)
        load_x(0, 2, 2)
        load_x(1)
        load_w2(1, 0)
        load_x(2)
        load_w2(1, 1)
        load_x(3)
        load_w3(0)
        load_w3(1)
        for r in range(4, AHEAD):
            load_x(r)

        ident = const.tile([P, P], F32, name="ident")
        make_identity(nc, ident[:])
        ident_bf = const.tile([P, 32], BF16, name="ident_bf")
        nc.gpsimd.tensor_copy(out=ident_bf[:], in_=ident[:, 0:32])

        bias2 = const.tile([P, 8], F32, name="bias2")
        b3bc = const.tile([P, 2, D_OUT], F32, name="b3bc")
        pbias = {}

        def bias_matmuls():
            pb = psum.tile([P, 512], F32, name="pb", tag="bank")
            nc.tensor.matmul(
                out=pb[:, 0:D_OUT], lhsT=halves[:], rhs=b3rows[:], start=True, stop=True
            )
            nc.tensor.matmul(
                out=pb[:, D_OUT : D_OUT + 32], lhsT=b2rows[:], rhs=ident_bf[:], start=True, stop=True
            )
            pbias[0] = pb

        def bias_copies():
            pb = pbias[0]
            nc.scalar.copy(out=bias2[:], in_=pb[:, D_OUT : D_OUT + 8])
            nc.scalar.copy(out=b3bc[:, 0, :], in_=pb[:, 0:D_OUT])
            nc.scalar.copy(out=b3bc[:, 1, :], in_=pb[:, 0:D_OUT])

        w2c = {}
        w2s = {}
        w3c = {}
        w3s = {}
        for t in range(T):
            w2c[t] = const.tile([P, 2, D_K], U32, name="w2c%d" % t, align_bytes=256)
            w2s[t] = const.tile([P, 2, D_K], U8, name="w2s%d" % t, align_bytes=256)
            w3c[t] = const.tile([P, D_OUT], U32, name="w3c%d" % t, align_bytes=256)
            w3s[t] = const.tile([P, D_OUT], U8, name="w3s%d" % t, align_bytes=256)

        grp2 = {}

        def regroup_w2(t, g):
            wg = wst.tile([P, 4 * D_K], BF16, name="wg", tag="wg", align_bytes=256)
            nc.vector.tensor_copy(
                out=wg[:].rearrange("p (c i t) -> p c t i", i=4, t=4),
                in_=w2raw[t][:, 4 * g : 4 * g + 4, :].rearrange("p t (c i) -> p c t i", i=4),
            )
            grp2[g] = wg

        def quant_w2(t, g):
            nc.vector.quantize_mx(
                out=w2c[t][:, g, :].bitcast(FP8X4), scales=w2s[t][:, g, :], in_=grp2[g][:]
            )

        def prep_w3():
            grp = {}
            for t in range(T):
                wg = wst.tile([P, 4 * D_OUT], BF16, name="wg3", tag="wg", align_bytes=256)
                nc.vector.tensor_copy(
                    out=wg[:].rearrange("p (c i t) -> p c t i", i=4, t=4),
                    in_=w3raw[t][:].rearrange("p t (c i) -> p c t i", i=4),
                )
                grp[t] = wg
            for t in range(T):
                nc.vector.quantize_mx(out=w3c[t][:].bitcast(FP8X4), scales=w3s[t][:], in_=grp[t][:])

        trb = {}
        ghs = {}
        hcs = {}
        h2ts = {}
        g2s = {}
        h2cs = {}
        pos = {}
        osb = {}

        def transposes(s):
            c, t, j0, nj = fronts[s]
            xw = xs[(c, t)][:].bitcast(F32)
            for g in range(2):
                for jb in range(0, nj, 2):
                    w = min(2, nj - jb)
                    bank = psum.tile([P, 2, 2 * P], F32, name="trb", tag="bank")
                    for u in range(2):
                        for jj in range(w):
                            col = (j0 + jb + jj) * 512 + g * 256 + u * 128
                            nc.tensor.transpose(
                                out=bank[:, u, jj * P : (jj + 1) * P],
                                in_=xw[:, col : col + P],
                                identity=ident[:],
                            )
                    trb[(s, g, jb)] = bank

        def exits_t(s):
            c, t, j0, nj = fronts[s]
            for g in range(2):
                gh = ghp.tile([P, 4 * CH], BF16, name="gh", tag="gh", align_bytes=256)
                ghs[(s, g)] = gh
                words = gh[:].bitcast(F32).rearrange("p (n u) -> p n u", u=2)
                for jb in range(0, nj, 2):
                    w = min(2, nj - jb)
                    dst = words[:, P * jb : P * (jb + w), :]
                    src = trb[(s, g, jb)][:, :, 0 : P * w].rearrange("p u n -> p n u")
                    if s in (7, 9, 11, 13) and g == 1 and jb == 2:
                        nc.vector.tensor_copy(out=dst, in_=src)
                    else:
                        nc.scalar.copy(out=dst, in_=src)

        def quant_h1(s):
            c, t, j0, nj = fronts[s]
            n = P * nj
            hc = hcp.tile([P, 2, CH], U32, name="hc", tag="hc", align_bytes=256)
            hs = hcp.tile([P, 2, CH], U8, name="hs", tag="hs", align_bytes=256)
            for j in range(j0, j0 + nj):
                hcs[(c, t, j)] = (hc, hs, P * (j - j0))
            for g in range(2):
                nc.vector.quantize_mx(
                    out=hc[:, g, 0:n].bitcast(FP8X4),
                    scales=hs[:, g, 0:n],
                    in_=ghs[(s, g)][:, 0 : 4 * n],
                )

        def stage1(s):
            c, t, j0, nj = backs[s]
            n = P * nj
            hc, hs, lo = hcs[(c, t, j0)]
            h2t = h2p.tile([P, 4, CH], BF16, name="h2t", tag="h2t", align_bytes=256)
            h2ts[s] = h2t
            for m in range(4):
                ps = psum.tile([P, CH], F32, name="ps1", tag="bank")
                for g in range(2):
                    nc.tensor.matmul_mx(
                        out=ps[:, 0:n],
                        lhsT=w2c[t][:, g, m * P : (m + 1) * P].bitcast(FP8X4),
                        lhsT_scale=w2s[t][:, g, m * P : (m + 1) * P],
                        rhs=hc[:, g, lo : lo + n].bitcast(FP8X4),
                        rhs_scale=hs[:, g, lo : lo + n],
                        start=(g == 0),
                        stop=(g == 1),
                    )
                nc.scalar.activation(
                    out=h2t[:, m, 0:n],
                    in_=ps[:, 0:n],
                    func=ACT.Relu,
                    bias=bias2[:, 4 * t + m : 4 * t + m + 1],
                    scale=1.0,
                )

        def parts(n):
            if n == P:
                return [(0, n)]
            return [(0, n // 2), (n // 2, n)]

        def regroup(s):
            n = P * backs[s][3]
            g2 = h2p.tile([P, 4 * CH], BF16, name="g2", tag="g2", align_bytes=256)
            copy = nc.scalar.copy if s >= n_backs - 2 else nc.vector.tensor_copy
            for lo, hi in parts(n):
                copy(
                    out=g2[:, 4 * lo : 4 * hi].rearrange("p (c i t) -> p c t i", i=4, t=4),
                    in_=h2ts[s][:, :, lo:hi].rearrange("p t (c i) -> p c t i", i=4),
                )
            g2s[s] = g2

        def quant_h2(s):
            c, t, j0, nj = backs[s]
            if j0 == 0:
                h2c = h2cp.tile([P, CH], U32, name="h2c", tag="h2c", align_bytes=256)
                h2s = h2cp.tile([P, CH], U8, name="h2s", tag="h2s", align_bytes=256)
                h2cs[(c, t)] = (h2c, h2s)
            h2c, h2s = h2cs[(c, t)]
            for lo, hi in parts(P * nj):
                nc.vector.quantize_mx(
                    out=h2c[:, P * j0 + lo : P * j0 + hi].bitcast(FP8X4),
                    scales=h2s[:, P * j0 + lo : P * j0 + hi],
                    in_=g2s[s][:, 4 * lo : 4 * hi],
                )

        def stage2(c, j0, w):
            po = psum.tile([P, 2, D_OUT], F32, name="po", tag="bank")
            for jj in range(w):
                j = j0 + jj
                for t in range(T):
                    h2c, h2s = h2cs[(c, t)]
                    nc.tensor.matmul_mx(
                        out=po[:, jj, :],
                        lhsT=h2c[:, j * P : (j + 1) * P].bitcast(FP8X4),
                        lhsT_scale=h2s[:, j * P : (j + 1) * P],
                        rhs=w3c[t][:].bitcast(FP8X4),
                        rhs_scale=w3s[t][:],
                        start=(t == 0),
                        stop=(t == T - 1),
                    )
            pos[(c, j0)] = po

        def exit_o(c, j0, w):
            if j0 == 0:
                o = outp.tile([P, 4, D_OUT], F32, name="o", tag="o")
                osb[c] = o
            nc.vector.scalar_tensor_tensor(
                out=osb[c][:, j0 : j0 + w, :],
                in0=pos[(c, j0)][:, 0:w, :],
                scalar=0.5,
                in1=b3bc[:, 0:w, :],
                op0=ALU.mult,
                op1=ALU.add,
            )
            rows = out[c * CH : (c + 1) * CH, :].rearrange("(p j) o -> p j o", j=4)
            if c >= NCH - 2:
                nc.sync.dma_start(out=rows[:, j0 : j0 + w, :], in_=osb[c][:, j0 : j0 + w, :])
            elif j0 + w == 4:
                nc.sync.dma_start(out=rows, in_=osb[c][:])

        bias_matmuls()
        bias_copies()
        regroup_w2(0, 0)
        regroup_w2(0, 1)
        quant_w2(0, 0)
        quant_w2(0, 1)
        due = []
        state = {"taken": 0, "pending": []}
        def step(s):
            taken = state["taken"]
            pending = state["pending"]
            if s + AHEAD < len(rounds):
                load_x(s + AHEAD)
            s1, s2 = s - 1, s - 2
            tail = s >= n_fronts
            if s < n_fronts:
                transposes(s)
            if s == 2:
                regroup_w2(1, 0)
            first = s == 3
            if first:
                exits_t(s)
                quant_h1(s)
            if 0 <= s2 < n_backs:
                regroup(s2)
            if pending and not tail:
                exit_o(pending[0][0], pending[0][1], pending[0][2])
                pending = pending[1:]
            if 0 <= s2 < n_backs:
                quant_h2(s2)
                c, t, j0, nj = backs[s2]
                if t == T - 1:
                    for jb in range(0, nj, 2):
                        due.append((c, j0 + jb, min(2, nj - jb), s))
            for c, j0, w in pending:
                exit_o(c, j0, w)
            pending = []
            if s < n_fronts and not first:
                exits_t(s)
            if 0 <= s1 < n_fronts - 1:
                stage1(s1)
            elif s1 == n_fronts - 1:
                for b in range(s1, n_backs):
                    stage1(b)
            if s < n_fronts and not first:
                quant_h1(s)
            if s == 2:
                regroup_w2(1, 1)
                quant_w2(1, 0)
                quant_w2(1, 1)
            if s == 4:
                prep_w3()
            while taken < len(due) and due[taken][3] < s and (tail or not pending):
                c, j0, w = due[taken][0:3]
                taken += 1
                stage2(c, j0, w)
                pending.append((c, j0, w))
            state["taken"] = taken
            state["pending"] = pending

        with tc.manual_schedule(engines={mybir.EngineType.DVE}):
            for s in range(HEAD_STEPS):
                step(s)
        for s in range(HEAD_STEPS, n_backs + 5):
            step(s)
